import numpy as np
import ml_dtypes

BF16 = ml_dtypes.bfloat16


def bf(x):
    return np.asarray(x, np.float32).astype(BF16)


def f32(x):
    return np.asarray(x, np.float32)


def f64(x):
    return np.asarray(x).astype(np.float64)


def striped(idx):
    return np.tile(idx.reshape(-1, 16).T, (8, 1))


C, S, N = 256, 256, 128


def ssp(v):
    return np.log(1.0 + np.exp(v)) - np.log(2.0)


def setup_inputs():
    return {"base": f32(np.random.standard_normal((C, S))), "x": f32(np.random.standard_normal((C, N))), "fbias": f32(1.5 + 0.5 * np.random.standard_normal((C, 1))), "w2": bf(np.random.standard_normal((C, C)) / np.sqrt(C)), "b2": f32(0.1 * np.random.standard_normal((C, 1))), "w3": bf(np.random.standard_normal((C, C)) / np.sqrt(C)), "b3": f32(0.1 * np.random.standard_normal((C, 1))), "offs": striped(np.random.permutation(S)[:N])}


def reference(base, x, fbias, w2, b2, w3, b3, offs):
    idx = offs[:16].T.reshape(-1)
    conv = ssp(f64(fbias)) * f64(x)
    h = ssp(f64(w2).T @ conv + f64(b2))
    res = f64(w3).T @ h + f64(b3)
    out = f64(base).copy()
    out[:, idx] = f64(x) + res
    return out

@@ -1,0 +1,95 @@
+import concourse.mybir as mybir
+
+F32 = mybir.dt.float32
+BF16 = mybir.dt.bfloat16
+U16 = mybir.dt.uint16
+FUNC = mybir.ActivationFunctionType
+ALU = mybir.AluOpType
+
+P = 128
+C, S, N = 256, 256, 128
+BLOCKS = C // P
+FLOPS = 2 * (2 * C * C * N)
+
+
+def tile_bouzidnet_kernel(tc, base, x, fbias, w2, b2, w3, b3, offs, out):
+    nc = tc.nc
+    with (
+        tc.tile_pool(name="held", bufs=1) as held,
+        tc.psum_pool(name="psum", bufs=1) as psum,
+    ):
+        offsets = held.tile([P, N // 16], U16, name="offsets")
+        fbias_t = held.tile([P, BLOCKS], F32, name="fbias_t")
+        b2_t = held.tile([P, BLOCKS], F32, name="b2_t")
+        b3_t = held.tile([P, BLOCKS], F32, name="b3_t")
+        x_t = held.tile([P, BLOCKS, N], F32, name="x_t")
+        w2_t = held.tile([P, BLOCKS, C], BF16, name="w2_t")
+        w3_t = held.tile([P, BLOCKS, C], BF16, name="w3_t")
+        windows = [held.tile([P, S], F32, name=f"window{c}") for c in range(BLOCKS)]
+
+        with nc.allow_non_contiguous_dma(reason="one float32 of a bias vector to a partition"):
+            nc.sync.dma_start(fbias_t[:], fbias.rearrange("(b p) o -> p (b o)", p=P))
+            nc.scalar.dma_start(b2_t[:], b2.rearrange("(b p) o -> p (b o)", p=P))
+            nc.gpsimd.dma_start(b3_t[:], b3.rearrange("(b p) o -> p (b o)", p=P))
+        nc.sync.dma_start(x_t[:], x.rearrange("(b p) n -> p b n", p=P))
+        nc.scalar.dma_start(w2_t[:], w2.rearrange("(b p) m -> p b m", p=P))
+        nc.gpsimd.dma_start(w3_t[:], w3.rearrange("(b p) c -> p b c", p=P))
+        nc.sync.dma_start(offsets[:], offs)
+        nc.sync.dma_start(windows[0][:], base[0:P, :])
+        nc.gpsimd.dma_start(windows[1][:], base[P : 2 * P, :])
+
+
+        f_abs = held.tile([P, BLOCKS], F32, name="f_abs")
+        f_exp = held.tile([P, BLOCKS], F32, name="f_exp")
+        f_log = held.tile([P, BLOCKS], F32, name="f_log")
+        f_relu2 = held.tile([P, BLOCKS], F32, name="f_relu2")
+        filt = held.tile([P, BLOCKS], F32, name="filt")
+        nc.scalar.activation(f_abs[:], fbias_t[:], FUNC.Abs)
+        nc.scalar.activation(f_exp[:], f_abs[:], FUNC.Exp, scale=-1.0)
+        nc.scalar.activation(f_log[:], f_exp[:], FUNC.Ln, bias=0.5, scale=0.5)
+        nc.vector.tensor_tensor(f_relu2[:], fbias_t[:], f_abs[:], ALU.add)
+        nc.vector.scalar_tensor_tensor(filt[:], f_relu2[:], 0.5, f_log[:], ALU.mult, ALU.add)
+
+        conv = held.tile([P, BLOCKS, N], BF16, name="conv")
+        for k in range(BLOCKS):
+            nc.vector.tensor_scalar(conv[:, k, :], x_t[:, k, :], filt[:, k : k + 1], None, ALU.mult)
+
+        pre = [psum.tile([P, N], F32, name=f"pre{m}") for m in range(BLOCKS)]
+        for m in range(BLOCKS):
+            for k in range(BLOCKS):
+                nc.tensor.matmul(
+                    pre[m][:], w2_t[:, k, m * P : (m + 1) * P], conv[:, k, :],
+                    start=(k == 0), stop=(k == BLOCKS - 1),
+                )
+
+        h_abs = held.tile([P, BLOCKS, N], F32, name="h_abs")
+        h_exp = held.tile([P, BLOCKS, N], F32, name="h_exp")
+        h_log = held.tile([P, BLOCKS, N], F32, name="h_log")
+        h_relu2 = held.tile([P, BLOCKS, N], F32, name="h_relu2")
+        h = held.tile([P, BLOCKS, N], BF16, name="h")
+        for m in range(BLOCKS):
+            nc.scalar.activation(h_abs[:, m, :], pre[m][:], FUNC.Abs, bias=b2_t[:, m : m + 1])
+        nc.scalar.activation(h_exp[:], h_abs[:], FUNC.Exp, scale=-1.0)
+        nc.scalar.activation(h_log[:], h_exp[:], FUNC.Ln, bias=0.5, scale=0.5)
+        for m in range(BLOCKS):
+            nc.vector.scalar_tensor_tensor(
+                h_relu2[:, m, :], pre[m][:], b2_t[:, m : m + 1], h_abs[:, m, :], ALU.add, ALU.add
+            )
+        nc.vector.scalar_tensor_tensor(h[:], h_relu2[:], 0.5, h_log[:], ALU.mult, ALU.add)
+
+        product = [psum.tile([P, N], F32, name=f"product{c}") for c in range(BLOCKS)]
+        res = held.tile([P, BLOCKS, N], F32, name="res")
+        for c in range(BLOCKS):
+            for m in range(BLOCKS):
+                nc.tensor.matmul(
+                    product[c][:], w3_t[:, m, c * P : (c + 1) * P], h[:, m, :],
+                    start=(m == 0), stop=(m == BLOCKS - 1),
+                )
+            nc.scalar.activation(
+                res[:, c, :], product[c][:], FUNC.Identity, bias=b3_t[:, c : c + 1]
+            )
+            nc.vector.tensor_tensor(
+                windows[c][:].indirect(offsets[:]), x_t[:, c, :], res[:, c, :], ALU.add
+            )
+        nc.sync.dma_start(out[0:P, :], windows[0][:])
+        nc.scalar.dma_start(out[P : 2 * P, :], windows[1][:])

@@ -11,6 +11,8 @@ C, S, N = 256, 256, 128
 BLOCKS = C // P
 FLOPS = 2 * (2 * C * C * N)
 
+CAP = 30.0
+
 
 def tile_bouzidnet_kernel(tc, base, x, fbias, w2, b2, w3, b3, offs, out):
     nc = tc.nc
@@ -39,16 +41,16 @@ def tile_bouzidnet_kernel(tc, base, x, fbias, w2, b2, w3, b3, offs, out):
         nc.gpsimd.dma_start(windows[1][:], base[P : 2 * P, :])
 
 
-        f_abs = held.tile([P, BLOCKS], F32, name="f_abs")
+        f_cap = held.tile([P, BLOCKS], F32, name="f_cap")
         f_exp = held.tile([P, BLOCKS], F32, name="f_exp")
         f_log = held.tile([P, BLOCKS], F32, name="f_log")
-        f_relu2 = held.tile([P, BLOCKS], F32, name="f_relu2")
+        f_over = held.tile([P, BLOCKS], F32, name="f_over")
         filt = held.tile([P, BLOCKS], F32, name="filt")
-        nc.scalar.activation(f_abs[:], fbias_t[:], FUNC.Abs)
-        nc.scalar.activation(f_exp[:], f_abs[:], FUNC.Exp, scale=-1.0)
+        nc.vector.tensor_scalar(f_cap[:], fbias_t[:], CAP, None, ALU.min)
+        nc.scalar.activation(f_exp[:], f_cap[:], FUNC.Exp)
         nc.scalar.activation(f_log[:], f_exp[:], FUNC.Ln, bias=0.5, scale=0.5)
-        nc.vector.tensor_tensor(f_relu2[:], fbias_t[:], f_abs[:], ALU.add)
-        nc.vector.scalar_tensor_tensor(filt[:], f_relu2[:], 0.5, f_log[:], ALU.mult, ALU.add)
+        nc.vector.tensor_tensor(f_over[:], fbias_t[:], f_cap[:], ALU.subtract)
+        nc.vector.tensor_tensor(filt[:], f_log[:], f_over[:], ALU.add)
 
         conv = held.tile([P, BLOCKS, N], BF16, name="conv")
         for k in range(BLOCKS):
@@ -62,20 +64,22 @@ def tile_bouzidnet_kernel(tc, base, x, fbias, w2, b2, w3, b3, offs, out):
                     start=(k == 0), stop=(k == BLOCKS - 1),
                 )
 
-        h_abs = held.tile([P, BLOCKS, N], F32, name="h_abs")
+        h_cap = held.tile([P, BLOCKS, N], F32, name="h_cap")
         h_exp = held.tile([P, BLOCKS, N], F32, name="h_exp")
         h_log = held.tile([P, BLOCKS, N], F32, name="h_log")
-        h_relu2 = held.tile([P, BLOCKS, N], F32, name="h_relu2")
+        h_over = held.tile([P, BLOCKS, N], F32, name="h_over")
         h = held.tile([P, BLOCKS, N], BF16, name="h")
         for m in range(BLOCKS):
-            nc.scalar.activation(h_abs[:, m, :], pre[m][:], FUNC.Abs, bias=b2_t[:, m : m + 1])
-        nc.scalar.activation(h_exp[:], h_abs[:], FUNC.Exp, scale=-1.0)
+            nc.vector.tensor_scalar(
+                h_cap[:, m, :], pre[m][:], b2_t[:, m : m + 1], CAP, ALU.add, ALU.min
+            )
+        nc.scalar.activation(h_exp[:], h_cap[:], FUNC.Exp)
         nc.scalar.activation(h_log[:], h_exp[:], FUNC.Ln, bias=0.5, scale=0.5)
         for m in range(BLOCKS):
             nc.vector.scalar_tensor_tensor(
-                h_relu2[:, m, :], pre[m][:], b2_t[:, m : m + 1], h_abs[:, m, :], ALU.add, ALU.add
+                h_over[:, m, :], pre[m][:], b2_t[:, m : m + 1], h_cap[:, m, :], ALU.add, ALU.subtract
             )
-        nc.vector.scalar_tensor_tensor(h[:], h_relu2[:], 0.5, h_log[:], ALU.mult, ALU.add)
+        nc.vector.tensor_tensor(h[:], h_log[:], h_over[:], ALU.add)
 
         product = [psum.tile([P, N], F32, name=f"product{c}") for c in range(BLOCKS)]
         res = held.tile([P, BLOCKS, N], F32, name="res")

@@ -12,6 +12,7 @@ BLOCKS = C // P
 FLOPS = 2 * (2 * C * C * N)
 
 CAP = 30.0
+EULER = 2.718281828459045
 
 
 def tile_bouzidnet_kernel(tc, base, x, fbias, w2, b2, w3, b3, offs, out):
@@ -31,14 +32,14 @@ def tile_bouzidnet_kernel(tc, base, x, fbias, w2, b2, w3, b3, offs, out):
 
         with nc.allow_non_contiguous_dma(reason="one float32 of a bias vector to a partition"):
             nc.sync.dma_start(fbias_t[:], fbias.rearrange("(b p) o -> p (b o)", p=P))
+            nc.sync.dma_start(x_t[:], x.rearrange("(b p) n -> p b n", p=P))
+            nc.scalar.dma_start(w2_t[:], w2.rearrange("(b p) m -> p b m", p=P))
             nc.scalar.dma_start(b2_t[:], b2.rearrange("(b p) o -> p (b o)", p=P))
-            nc.gpsimd.dma_start(b3_t[:], b3.rearrange("(b p) o -> p (b o)", p=P))
-        nc.sync.dma_start(x_t[:], x.rearrange("(b p) n -> p b n", p=P))
-        nc.scalar.dma_start(w2_t[:], w2.rearrange("(b p) m -> p b m", p=P))
-        nc.gpsimd.dma_start(w3_t[:], w3.rearrange("(b p) c -> p b c", p=P))
-        nc.sync.dma_start(offsets[:], offs)
-        nc.sync.dma_start(windows[0][:], base[0:P, :])
-        nc.gpsimd.dma_start(windows[1][:], base[P : 2 * P, :])
+            nc.gpsimd.dma_start(w3_t[:], w3.rearrange("(b p) c -> p b c", p=P))
+            nc.sync.dma_start(offsets[:], offs)
+            nc.sync.dma_start(b3_t[:], b3.rearrange("(b p) o -> p (b o)", p=P))
+            nc.sync.dma_start(windows[0][:], base[0:P, :])
+            nc.sync.dma_start(windows[1][:], base[P : 2 * P, :])
 
 
         f_cap = held.tile([P, BLOCKS], F32, name="f_cap")
@@ -46,8 +47,10 @@ def tile_bouzidnet_kernel(tc, base, x, fbias, w2, b2, w3, b3, offs, out):
         f_log = held.tile([P, BLOCKS], F32, name="f_log")
         f_over = held.tile([P, BLOCKS], F32, name="f_over")
         filt = held.tile([P, BLOCKS], F32, name="filt")
+        euler = held.tile([P, BLOCKS], F32, name="euler")
+        nc.gpsimd.memset(euler[:], EULER)
         nc.vector.tensor_scalar(f_cap[:], fbias_t[:], CAP, None, ALU.min)
-        nc.scalar.activation(f_exp[:], f_cap[:], FUNC.Exp)
+        nc.gpsimd.tensor_tensor(f_exp[:], euler[:], f_cap[:], ALU.pow)
         nc.scalar.activation(f_log[:], f_exp[:], FUNC.Ln, bias=0.5, scale=0.5)
         nc.vector.tensor_tensor(f_over[:], fbias_t[:], f_cap[:], ALU.subtract)
         nc.vector.tensor_tensor(filt[:], f_log[:], f_over[:], ALU.add)
@@ -57,8 +60,8 @@ def tile_bouzidnet_kernel(tc, base, x, fbias, w2, b2, w3, b3, offs, out):
             nc.vector.tensor_scalar(conv[:, k, :], x_t[:, k, :], filt[:, k : k + 1], None, ALU.mult)
 
         pre = [psum.tile([P, N], F32, name=f"pre{m}") for m in range(BLOCKS)]
-        for m in range(BLOCKS):
-            for k in range(BLOCKS):
+        for k in range(BLOCKS):
+            for m in range(BLOCKS):
                 nc.tensor.matmul(
                     pre[m][:], w2_t[:, k, m * P : (m + 1) * P], conv[:, k, :],
                     start=(k == 0), stop=(k == BLOCKS - 1),
@@ -73,22 +76,26 @@ def tile_bouzidnet_kernel(tc, base, x, fbias, w2, b2, w3, b3, offs, out):
             nc.vector.tensor_scalar(
                 h_cap[:, m, :], pre[m][:], b2_t[:, m : m + 1], CAP, ALU.add, ALU.min
             )
-        nc.scalar.activation(h_exp[:], h_cap[:], FUNC.Exp)
-        nc.scalar.activation(h_log[:], h_exp[:], FUNC.Ln, bias=0.5, scale=0.5)
+        for m in range(BLOCKS):
+            nc.scalar.activation(h_exp[:, m, :], h_cap[:, m, :], FUNC.Exp)
+        for m in range(BLOCKS):
+            nc.scalar.activation(h_log[:, m, :], h_exp[:, m, :], FUNC.Ln, bias=0.5, scale=0.5)
         for m in range(BLOCKS):
             nc.vector.scalar_tensor_tensor(
                 h_over[:, m, :], pre[m][:], b2_t[:, m : m + 1], h_cap[:, m, :], ALU.add, ALU.subtract
             )
-        nc.vector.tensor_tensor(h[:], h_log[:], h_over[:], ALU.add)
+        for m in range(BLOCKS):
+            nc.vector.tensor_tensor(h[:, m, :], h_log[:, m, :], h_over[:, m, :], ALU.add)
 
         product = [psum.tile([P, N], F32, name=f"product{c}") for c in range(BLOCKS)]
         res = held.tile([P, BLOCKS, N], F32, name="res")
-        for c in range(BLOCKS):
-            for m in range(BLOCKS):
+        for m in range(BLOCKS):
+            for c in range(BLOCKS):
                 nc.tensor.matmul(
                     product[c][:], w3_t[:, m, c * P : (c + 1) * P], h[:, m, :],
                     start=(m == 0), stop=(m == BLOCKS - 1),
                 )
+        for c in range(BLOCKS):
             nc.scalar.activation(
                 res[:, c, :], product[c][:], FUNC.Identity, bias=b3_t[:, c : c + 1]
             )

@@ -9,6 +9,7 @@ ALU = mybir.AluOpType
 P = 128
 C, S, N = 256, 256, 128
 BLOCKS = C // P
+PAD = 8
 FLOPS = 2 * (2 * C * C * N)
 
 CAP = 30.0
@@ -22,7 +23,8 @@ def tile_bouzidnet_kernel(tc, base, x, fbias, w2, b2, w3, b3, offs, out):
         tc.psum_pool(name="psum", bufs=1) as psum,
     ):
         offsets = held.tile([P, N // 16], U16, name="offsets")
-        fbias_t = held.tile([P, BLOCKS], F32, name="fbias_t")
+        fbias_pad = held.tile([P, BLOCKS, PAD], F32, name="fbias_pad")
+        fbias_t = fbias_pad[:, :, 0]
         b2_t = held.tile([P, BLOCKS], F32, name="b2_t")
         b3_t = held.tile([P, BLOCKS], F32, name="b3_t")
         x_t = held.tile([P, BLOCKS, N], F32, name="x_t")
@@ -31,7 +33,7 @@ def tile_bouzidnet_kernel(tc, base, x, fbias, w2, b2, w3, b3, offs, out):
         windows = [held.tile([P, S], F32, name=f"window{c}") for c in range(BLOCKS)]
 
         with nc.allow_non_contiguous_dma(reason="one float32 of a bias vector to a partition"):
-            nc.sync.dma_start(fbias_t[:], fbias.rearrange("(b p) o -> p (b o)", p=P))
+            nc.sync.dma_start(fbias_pad[:, :, 0:1], fbias.rearrange("(b p) o -> p b o", p=P))
             nc.sync.dma_start(x_t[:], x.rearrange("(b p) n -> p b n", p=P))
             nc.scalar.dma_start(w2_t[:], w2.rearrange("(b p) m -> p b m", p=P))
             nc.scalar.dma_start(b2_t[:], b2.rearrange("(b p) o -> p (b o)", p=P))
@@ -49,10 +51,10 @@ def tile_bouzidnet_kernel(tc, base, x, fbias, w2, b2, w3, b3, offs, out):
         filt = held.tile([P, BLOCKS], F32, name="filt")
         euler = held.tile([P, BLOCKS], F32, name="euler")
         nc.gpsimd.memset(euler[:], EULER)
-        nc.vector.tensor_scalar(f_cap[:], fbias_t[:], CAP, None, ALU.min)
+        nc.vector.tensor_scalar(f_cap[:], fbias_t, CAP, None, ALU.min)
         nc.gpsimd.tensor_tensor(f_exp[:], euler[:], f_cap[:], ALU.pow)
         nc.scalar.activation(f_log[:], f_exp[:], FUNC.Ln, bias=0.5, scale=0.5)
-        nc.vector.tensor_tensor(f_over[:], fbias_t[:], f_cap[:], ALU.subtract)
+        nc.vector.tensor_tensor(f_over[:], fbias_t, f_cap[:], ALU.subtract)
         nc.vector.tensor_tensor(filt[:], f_log[:], f_over[:], ALU.add)
 
         conv = held.tile([P, BLOCKS, N], BF16, name="conv")

@@ -9,7 +9,6 @@ ALU = mybir.AluOpType
 P = 128
 C, S, N = 256, 256, 128
 BLOCKS = C // P
-PAD = 8
 FLOPS = 2 * (2 * C * C * N)
 
 CAP = 30.0
@@ -23,8 +22,7 @@ def tile_bouzidnet_kernel(tc, base, x, fbias, w2, b2, w3, b3, offs, out):
         tc.psum_pool(name="psum", bufs=1) as psum,
     ):
         offsets = held.tile([P, N // 16], U16, name="offsets")
-        fbias_pad = held.tile([P, BLOCKS, PAD], F32, name="fbias_pad")
-        fbias_t = fbias_pad[:, :, 0]
+        fbias_t = held.tile([P, BLOCKS], F32, name="fbias_t")
         b2_t = held.tile([P, BLOCKS], F32, name="b2_t")
         b3_t = held.tile([P, BLOCKS], F32, name="b3_t")
         x_t = held.tile([P, BLOCKS, N], F32, name="x_t")
@@ -33,12 +31,12 @@ def tile_bouzidnet_kernel(tc, base, x, fbias, w2, b2, w3, b3, offs, out):
         windows = [held.tile([P, S], F32, name=f"window{c}") for c in range(BLOCKS)]
 
         with nc.allow_non_contiguous_dma(reason="one float32 of a bias vector to a partition"):
-            nc.sync.dma_start(fbias_pad[:, :, 0:1], fbias.rearrange("(b p) o -> p b o", p=P))
-            nc.sync.dma_start(x_t[:], x.rearrange("(b p) n -> p b n", p=P))
+            nc.sync.dma_start(fbias_t[:], fbias.rearrange("(b p) o -> p (b o)", p=P))
+            nc.scalar.dma_start(x_t[:], x.rearrange("(b p) n -> p b n", p=P))
             nc.scalar.dma_start(w2_t[:], w2.rearrange("(b p) m -> p b m", p=P))
-            nc.scalar.dma_start(b2_t[:], b2.rearrange("(b p) o -> p (b o)", p=P))
-            nc.gpsimd.dma_start(w3_t[:], w3.rearrange("(b p) c -> p b c", p=P))
+            nc.sync.dma_start(b2_t[:], b2.rearrange("(b p) o -> p (b o)", p=P))
             nc.sync.dma_start(offsets[:], offs)
+            nc.sync.dma_start(w3_t[:], w3.rearrange("(b p) c -> p b c", p=P))
             nc.sync.dma_start(b3_t[:], b3.rearrange("(b p) o -> p (b o)", p=P))
             nc.sync.dma_start(windows[0][:], base[0:P, :])
             nc.sync.dma_start(windows[1][:], base[P : 2 * P, :])
@@ -51,10 +49,10 @@ def tile_bouzidnet_kernel(tc, base, x, fbias, w2, b2, w3, b3, offs, out):
         filt = held.tile([P, BLOCKS], F32, name="filt")
         euler = held.tile([P, BLOCKS], F32, name="euler")
         nc.gpsimd.memset(euler[:], EULER)
-        nc.vector.tensor_scalar(f_cap[:], fbias_t, CAP, None, ALU.min)
+        nc.vector.tensor_scalar(f_cap[:], fbias_t[:], CAP, None, ALU.min)
         nc.gpsimd.tensor_tensor(f_exp[:], euler[:], f_cap[:], ALU.pow)
         nc.scalar.activation(f_log[:], f_exp[:], FUNC.Ln, bias=0.5, scale=0.5)
-        nc.vector.tensor_tensor(f_over[:], fbias_t, f_cap[:], ALU.subtract)
+        nc.vector.tensor_tensor(f_over[:], fbias_t[:], f_cap[:], ALU.subtract)
         nc.vector.tensor_tensor(filt[:], f_log[:], f_over[:], ALU.add)
 
         conv = held.tile([P, BLOCKS, N], BF16, name="conv")

@@ -26,20 +26,21 @@ def tile_bouzidnet_kernel(tc, base, x, fbias, w2, b2, w3, b3, offs, out):
         b2_t = held.tile([P, BLOCKS], F32, name="b2_t")
         b3_t = held.tile([P, BLOCKS], F32, name="b3_t")
         x_t = held.tile([P, BLOCKS, N], F32, name="x_t")
-        w2_t = held.tile([P, BLOCKS, C], BF16, name="w2_t")
-        w3_t = held.tile([P, BLOCKS, C], BF16, name="w3_t")
+        w2_t = held.tile([P, BLOCKS, P, BLOCKS], BF16, name="w2_t")
+        w3_t = held.tile([P, BLOCKS, P, BLOCKS], BF16, name="w3_t")
         windows = [held.tile([P, S], F32, name=f"window{c}") for c in range(BLOCKS)]
 
-        with nc.allow_non_contiguous_dma(reason="one float32 of a bias vector to a partition"):
-            nc.sync.dma_start(fbias_t[:], fbias.rearrange("(b p) o -> p (b o)", p=P))
-            nc.scalar.dma_start(x_t[:], x.rearrange("(b p) n -> p b n", p=P))
-            nc.scalar.dma_start(w2_t[:], w2.rearrange("(b p) m -> p b m", p=P))
-            nc.sync.dma_start(b2_t[:], b2.rearrange("(b p) o -> p (b o)", p=P))
-            nc.sync.dma_start(offsets[:], offs)
-            nc.sync.dma_start(w3_t[:], w3.rearrange("(b p) c -> p b c", p=P))
-            nc.sync.dma_start(b3_t[:], b3.rearrange("(b p) o -> p (b o)", p=P))
-            nc.sync.dma_start(windows[0][:], base[0:P, :])
-            nc.sync.dma_start(windows[1][:], base[P : 2 * P, :])
+        base_blocks = base.rearrange("(p b) s -> p b s", b=BLOCKS)
+        out_blocks = out.rearrange("(p b) s -> p b s", b=BLOCKS)
+        nc.sync.dma_start(fbias_t[:], fbias.rearrange("(p b) o -> p (b o)", b=BLOCKS))
+        nc.scalar.dma_start(x_t[:], x.rearrange("(p b) n -> p b n", b=BLOCKS))
+        nc.scalar.dma_start(w2_t[:], w2.rearrange("(p k) (q m) -> p k q m", k=BLOCKS, m=BLOCKS))
+        nc.sync.dma_start(b2_t[:], b2.rearrange("(p b) o -> p (b o)", b=BLOCKS))
+        nc.sync.dma_start(offsets[:], offs)
+        nc.sync.dma_start(w3_t[:], w3.rearrange("(p m) (q c) -> p m q c", m=BLOCKS, c=BLOCKS))
+        nc.sync.dma_start(b3_t[:], b3.rearrange("(p b) o -> p (b o)", b=BLOCKS))
+        nc.sync.dma_start(windows[0][:], base_blocks[:, 0, :])
+        nc.sync.dma_start(windows[1][:], base_blocks[:, 1, :])
 
 
         f_cap = held.tile([P, BLOCKS], F32, name="f_cap")
@@ -63,7 +64,7 @@ def tile_bouzidnet_kernel(tc, base, x, fbias, w2, b2, w3, b3, offs, out):
         for k in range(BLOCKS):
             for m in range(BLOCKS):
                 nc.tensor.matmul(
-                    pre[m][:], w2_t[:, k, m * P : (m + 1) * P], conv[:, k, :],
+                    pre[m][:], w2_t[:, k, :, m], conv[:, k, :],
                     start=(k == 0), stop=(k == BLOCKS - 1),
                 )
 
@@ -92,7 +93,7 @@ def tile_bouzidnet_kernel(tc, base, x, fbias, w2, b2, w3, b3, offs, out):
         for m in range(BLOCKS):
             for c in range(BLOCKS):
                 nc.tensor.matmul(
-                    product[c][:], w3_t[:, m, c * P : (c + 1) * P], h[:, m, :],
+                    product[c][:], w3_t[:, m, :, c], h[:, m, :],
                     start=(m == 0), stop=(m == BLOCKS - 1),
                 )
         for c in range(BLOCKS):
@@ -102,5 +103,5 @@ def tile_bouzidnet_kernel(tc, base, x, fbias, w2, b2, w3, b3, offs, out):
             nc.vector.tensor_tensor(
                 windows[c][:].indirect(offsets[:]), x_t[:, c, :], res[:, c, :], ALU.add
             )
-        nc.sync.dma_start(out[0:P, :], windows[0][:])
-        nc.scalar.dma_start(out[P : 2 * P, :], windows[1][:])
+        nc.sync.dma_start(out_blocks[:, 0, :], windows[0][:])
+        nc.scalar.dma_start(out_blocks[:, 1, :], windows[1][:])

import concourse.mybir as mybir

F32 = mybir.dt.float32
BF16 = mybir.dt.bfloat16
U16 = mybir.dt.uint16
FUNC = mybir.ActivationFunctionType
ALU = mybir.AluOpType

P = 128
C, S, N = 256, 256, 128
BLOCKS = C // P
FLOPS = 2 * (2 * C * C * N)

CAP = 30.0
EULER = 2.718281828459045


def tile_bouzidnet_kernel(tc, base, x, fbias, w2, b2, w3, b3, offs, out):
    nc = tc.nc
    with (
        tc.tile_pool(name="held", bufs=1) as held,
        tc.psum_pool(name="psum", bufs=1) as psum,
    ):
        offsets = held.tile([P, N // 16], U16, name="offsets")
        fbias_t = held.tile([P, BLOCKS], F32, name="fbias_t")
        b2_t = held.tile([P, BLOCKS], F32, name="b2_t")
        b3_t = held.tile([P, BLOCKS], F32, name="b3_t")
        x_t = held.tile([P, BLOCKS, N], F32, name="x_t")
        w2_t = held.tile([P, BLOCKS, P, BLOCKS], BF16, name="w2_t")
        w3_t = held.tile([P, BLOCKS, P, BLOCKS], BF16, name="w3_t")
        windows = [held.tile([P, S], F32, name=f"window{c}") for c in range(BLOCKS)]

        base_blocks = base.rearrange("(p b) s -> p b s", b=BLOCKS)
        out_blocks = out.rearrange("(p b) s -> p b s", b=BLOCKS)
        nc.sync.dma_start(fbias_t[:], fbias.rearrange("(p b) o -> p (b o)", b=BLOCKS))
        nc.scalar.dma_start(x_t[:], x.rearrange("(p b) n -> p b n", b=BLOCKS))
        nc.scalar.dma_start(w2_t[:], w2.rearrange("(p k) (q m) -> p k q m", k=BLOCKS, m=BLOCKS))
        nc.sync.dma_start(b2_t[:], b2.rearrange("(p b) o -> p (b o)", b=BLOCKS))
        nc.sync.dma_start(offsets[:], offs)
        nc.sync.dma_start(w3_t[:], w3.rearrange("(p m) (q c) -> p m q c", m=BLOCKS, c=BLOCKS))
        nc.sync.dma_start(b3_t[:], b3.rearrange("(p b) o -> p (b o)", b=BLOCKS))
        nc.sync.dma_start(windows[0][:], base_blocks[:, 0, :])
        nc.sync.dma_start(windows[1][:], base_blocks[:, 1, :])


        f_cap = held.tile([P, BLOCKS], F32, name="f_cap")
        f_exp = held.tile([P, BLOCKS], F32, name="f_exp")
        f_log = held.tile([P, BLOCKS], F32, name="f_log")
        f_over = held.tile([P, BLOCKS], F32, name="f_over")
        filt = held.tile([P, BLOCKS], F32, name="filt")
        euler = held.tile([P, BLOCKS], F32, name="euler")
        nc.gpsimd.memset(euler[:], EULER)
        nc.vector.tensor_scalar(f_cap[:], fbias_t[:], CAP, None, ALU.min)
        nc.gpsimd.tensor_tensor(f_exp[:], euler[:], f_cap[:], ALU.pow)
        nc.scalar.activation(f_log[:], f_exp[:], FUNC.Ln, bias=0.5, scale=0.5)
        nc.vector.tensor_tensor(f_over[:], fbias_t[:], f_cap[:], ALU.subtract)
        nc.vector.tensor_tensor(filt[:], f_log[:], f_over[:], ALU.add)

        conv = held.tile([P, BLOCKS, N], BF16, name="conv")
        for k in range(BLOCKS):
            nc.vector.tensor_scalar(conv[:, k, :], x_t[:, k, :], filt[:, k : k + 1], None, ALU.mult)

        pre = [psum.tile([P, N], F32, name=f"pre{m}") for m in range(BLOCKS)]
        for k in range(BLOCKS):
            for m in range(BLOCKS):
                nc.tensor.matmul(
                    pre[m][:], w2_t[:, k, :, m], conv[:, k, :],
                    start=(k == 0), stop=(k == BLOCKS - 1),
                )

        h_cap = held.tile([P, BLOCKS, N], F32, name="h_cap")
        h_exp = held.tile([P, BLOCKS, N], F32, name="h_exp")
        h_log = held.tile([P, BLOCKS, N], F32, name="h_log")
        h_over = held.tile([P, BLOCKS, N], F32, name="h_over")
        h = held.tile([P, BLOCKS, N], BF16, name="h")
        for m in range(BLOCKS):
            nc.vector.tensor_scalar(
                h_cap[:, m, :], pre[m][:], b2_t[:, m : m + 1], CAP, ALU.add, ALU.min
            )
        for m in range(BLOCKS):
            nc.scalar.activation(h_exp[:, m, :], h_cap[:, m, :], FUNC.Exp)
        for m in range(BLOCKS):
            nc.scalar.activation(h_log[:, m, :], h_exp[:, m, :], FUNC.Ln, bias=0.5, scale=0.5)
        for m in range(BLOCKS):
            nc.vector.scalar_tensor_tensor(
                h_over[:, m, :], pre[m][:], b2_t[:, m : m + 1], h_cap[:, m, :], ALU.add, ALU.subtract
            )
        for m in range(BLOCKS):
            nc.vector.tensor_tensor(h[:, m, :], h_log[:, m, :], h_over[:, m, :], ALU.add)

        product = [psum.tile([P, N], F32, name=f"product{c}") for c in range(BLOCKS)]
        res = held.tile([P, BLOCKS, N], F32, name="res")
        for m in range(BLOCKS):
            for c in range(BLOCKS):
                nc.tensor.matmul(
                    product[c][:], w3_t[:, m, :, c], h[:, m, :],
                    start=(m == 0), stop=(m == BLOCKS - 1),
                )
        for c in range(BLOCKS):
            nc.scalar.activation(
                res[:, c, :], product[c][:], FUNC.Identity, bias=b3_t[:, c : c + 1]
            )
            nc.vector.tensor_tensor(
                windows[c][:].indirect(offsets[:]), x_t[:, c, :], res[:, c, :], ALU.add
            )
        nc.sync.dma_start(out_blocks[:, 0, :], windows[0][:])
        nc.scalar.dma_start(out_blocks[:, 1, :], windows[1][:])
